import numpy as np
import ml_dtypes


def mxq(x, axis, fmt="e4m3"):
    dtype, down = {"e4m3": (ml_dtypes.float8_e4m3fn, 7), "e5m2": (ml_dtypes.float8_e5m2, 14)}[fmt]
    v = np.moveaxis(np.asarray(x, np.float32).astype(ml_dtypes.bfloat16).astype(np.float64), axis, -1)
    blocks = v.reshape(v.shape[:-1] + (-1, 32))
    amax = np.abs(blocks).max(-1, keepdims=True)
    byte = np.maximum(np.where(amax > 0, np.frexp(amax)[1] - 1 + 127, 0) - down, 1)
    scale = np.exp2(byte - 127.0)
    codes = (blocks / scale).astype(np.float32).astype(dtype).astype(np.float64)
    return np.moveaxis((codes * scale).reshape(v.shape), -1, axis)


WIDE = False


def mx_kscale(k):
    if not WIDE:
        return np.ones(k)
    levels = np.array([10, -10, 5, -5, 0])
    a = np.random.permutation(np.resize(levels, k // 512 * 4)).reshape(k // 512, 4)
    idx = np.arange(k)
    return np.exp2(a[idx // 512, idx % 128 // 32])


BF16 = ml_dtypes.bfloat16


def bf(x):
    return np.asarray(x, np.float32).astype(BF16)


def f64(x):
    return np.asarray(x).astype(np.float64)


B, C, O, ROWS, COLS, KH, KW = 128, 1024, 128, 2, 2, 4, 4
H, W, K = ROWS + KH - 1, COLS + KW - 1, C * KH * KW


def setup_inputs():
    sc = mx_kscale(K)[::KH * KW]
    return {"x": bf(np.random.standard_normal((B, C, H, W)) * sc[None, :, None, None]),
            "weight": bf(np.random.standard_normal((ROWS, COLS, O, C, KH, KW)) / np.sqrt(K) / sc[None, None, None, :, None, None])}


def reference(x, weight):
    x, weight = f64(x), f64(weight)
    rows, cols, o, c, kh, kw = weight.shape
    b = x.shape[0]
    patches = np.stack(
        [np.stack([x[:, :, u:u + rows, v:v + cols] for v in range(kw)], axis=2)
         for u in range(kh)], axis=2)
    p = patches.transpose(4, 5, 0, 1, 2, 3).reshape(rows * cols, b, c * kh * kw)
    w = weight.reshape(rows * cols, o, c * kh * kw)
    y = mxq(p, 2, "e4m3") @ mxq(w, 2, "e4m3").transpose(0, 2, 1)
    return y.reshape(rows, cols, b, o).transpose(2, 3, 0, 1)

@@ -1,0 +1,148 @@
+from contextlib import ExitStack
+
+import concourse.mybir as mybir
+from concourse.masks import make_identity
+
+BF16 = mybir.dt.bfloat16
+F32 = mybir.dt.float32
+U32 = mybir.dt.uint32
+U8 = mybir.dt.uint8
+FP8X4 = mybir.dt.float8_e4m3fn_x4
+
+P = 128
+CHANNELS = 1024
+ROWS = 2
+COLS = 2
+KH = 4
+KW = 4
+HEIGHT = ROWS + KH - 1
+WIDTH = COLS + KW - 1
+POSITIONS = ROWS * COLS
+
+CHUNK_CHANNELS = 128
+CHUNKS = CHANNELS // CHUNK_CHANNELS
+CHUNK_K = CHUNK_CHANNELS * KH * KW
+CHUNK_X = CHUNK_CHANNELS * HEIGHT * WIDTH
+K_PASS = 4 * P
+PASSES = CHUNK_K // K_PASS
+BANK_WORDS = 512
+BANK_FLIPS = BANK_WORDS // P
+BANK_PASSES = BANK_FLIPS // 2
+ROUND_BANKS = PASSES // BANK_PASSES
+ROUNDS = CHUNKS * POSITIONS
+
+FLOPS = 2 * POSITIONS * P * P * CHANNELS * KH * KW
+
+
+def flip(nc, banks, identity, rows, grouped):
+    row_words = rows[:].bitcast(F32)
+    grouped_words = grouped[:].bitcast(F32)
+    for n in range(ROUND_BANKS):
+        bank = banks.tile([P, BANK_FLIPS, P], F32)
+        for f in range(BANK_FLIPS):
+            first = (n * BANK_FLIPS + f) * P
+            nc.tensor.transpose(bank[:, f, :], row_words[:, first : first + P], identity[:])
+        nc.scalar.copy(
+            out=grouped_words[:, n * BANK_WORDS : (n + 1) * BANK_WORDS].rearrange(
+                "p (g c h) -> p g c h", g=BANK_PASSES, h=2
+            ),
+            in_=bank[:].rearrange("p (g h) c -> p g c h", h=2),
+        )
+
+
+def quantise(nc, pool, grouped, label):
+    codes = pool.tile([P, CHUNK_K // 4], U32, name=label + "_codes", tag=label + "_codes", align_bytes=64)
+    scales = pool.tile([P, CHUNK_K // 4], U8, name=label + "_scales", tag=label + "_scales", align_bytes=64)
+    nc.vector.quantize_mx(out=codes[:].bitcast(FP8X4), scales=scales[:], in_=grouped[:])
+    return codes, scales
+
+
+def tile_localconvolution_k_kernel(tc, x, weight, out):
+    nc = tc.nc
+    with ExitStack() as ctx:
+        const = ctx.enter_context(tc.tile_pool(name="const", bufs=1))
+        inputs = ctx.enter_context(tc.tile_pool(name="inputs", bufs=1))
+        patches = ctx.enter_context(tc.tile_pool(name="patches", bufs=3))
+        regrouped = ctx.enter_context(tc.tile_pool(name="regrouped", bufs=2))
+        quantised = ctx.enter_context(tc.tile_pool(name="quantised", bufs=3))
+        banks = ctx.enter_context(tc.psum_pool(name="banks", bufs=4))
+        sums = ctx.enter_context(tc.psum_pool(name="sums", bufs=1))
+        ctx.enter_context(tc.manual_schedule())
+
+        identity = const.tile([P, P], F32)
+        make_identity(nc, identity[:])
+
+        x_chunks = []
+        w_chunks = []
+        for c in range(CHUNKS):
+            channels = slice(c * CHUNK_CHANNELS, (c + 1) * CHUNK_CHANNELS)
+            x_sb = inputs.tile([P, CHUNK_X], BF16, name="x%d" % c)
+            nc.sync.dma_start(out=x_sb[:], in_=x[:, channels, :, :].rearrange("b c h w -> b (c h w)"))
+            x_chunks.append(x_sb)
+            for q in range(POSITIONS):
+                w_sb = inputs.tile([P, CHUNK_K], BF16, name="w%d_%d" % (c, q))
+                nc.sync.dma_start(
+                    out=w_sb[:],
+                    in_=weight[q // COLS, q % COLS, :, channels, :, :].rearrange("o c u v -> o (c u v)"),
+                )
+                w_chunks.append(w_sb)
+
+        totals = [sums.tile([P, P], F32, name="total%d" % q) for q in range(POSITIONS)]
+        planes = const.tile([P, POSITIONS, P], F32)
+
+        def gather(r):
+            i = (r % POSITIONS) // COLS
+            j = (r % POSITIONS) % COLS
+            patch = patches.tile([P, CHUNK_K], BF16)
+            nc.vector.tensor_copy(
+                out=patch[:].rearrange("b (c u v) -> b c u v", u=KH, v=KW),
+                in_=x_chunks[r // POSITIONS][:].rearrange("b (c h w) -> b c h w", h=HEIGHT, w=WIDTH)[
+                    :, :, i : i + KH, j : j + KW
+                ],
+            )
+            return patch
+
+        def transpose(r, patch):
+            w_grouped = regrouped.tile([P, CHUNK_K], BF16, align_bytes=64)
+            flip(nc, banks, identity, w_chunks[r], w_grouped)
+            x_grouped = regrouped.tile([P, CHUNK_K], BF16, align_bytes=64)
+            flip(nc, banks, identity, patch, x_grouped)
+            return x_grouped, w_grouped
+
+        def multiply(r, x_mx, w_mx):
+            x_codes, x_scales = x_mx
+            w_codes, w_scales = w_mx
+            for g in range(PASSES):
+                cols = slice(g * P, (g + 1) * P)
+                nc.tensor.matmul_mx(
+                    out=totals[r % POSITIONS][:],
+                    lhsT=x_codes[:, cols].bitcast(FP8X4),
+                    lhsT_scale=x_scales[:, cols],
+                    rhs=w_codes[:, cols].bitcast(FP8X4),
+                    rhs_scale=w_scales[:, cols],
+                    start=(r // POSITIONS == 0 and g == 0),
+                    stop=(r // POSITIONS == CHUNKS - 1 and g == PASSES - 1),
+                )
+            if r // POSITIONS == CHUNKS - 1:
+                nc.vector.tensor_copy(out=planes[:, r % POSITIONS, :], in_=totals[r % POSITIONS][:])
+
+        patch_of = {0: gather(0)}
+        grouped_of = {}
+        mx_of = {}
+        for s in range(ROUNDS + 2):
+            if s + 1 < ROUNDS:
+                patch_of[s + 1] = gather(s + 1)
+            if s < ROUNDS:
+                grouped_of[s] = transpose(s, patch_of[s])
+            if 1 <= s <= ROUNDS:
+                x_grouped, w_grouped = grouped_of[s - 1]
+                w_mx = quantise(nc, quantised, w_grouped, "w")
+                x_mx = quantise(nc, quantised, x_grouped, "x")
+                mx_of[s - 1] = (x_mx, w_mx)
+            if s >= 2:
+                x_mx, w_mx = mx_of[s - 2]
+                multiply(s - 2, x_mx, w_mx)
+
+        result = const.tile([P, P, POSITIONS], F32)
+        nc.vector.tensor_copy(out=result[:], in_=planes[:].rearrange("b q o -> b o q"))
+        nc.sync.dma_start(out=out.rearrange("b o i j -> b (o i j)"), in_=result[:].rearrange("b o q -> b (o q)"))

@@ -19,42 +19,21 @@ HEIGHT = ROWS + KH - 1
 WIDTH = COLS + KW - 1
 POSITIONS = ROWS * COLS
 
-CHUNK_CHANNELS = 128
-CHUNKS = CHANNELS // CHUNK_CHANNELS
-CHUNK_K = CHUNK_CHANNELS * KH * KW
-CHUNK_X = CHUNK_CHANNELS * HEIGHT * WIDTH
 K_PASS = 4 * P
-PASSES = CHUNK_K // K_PASS
 BANK_WORDS = 512
-BANK_FLIPS = BANK_WORDS // P
-BANK_PASSES = BANK_FLIPS // 2
-ROUND_BANKS = PASSES // BANK_PASSES
+UNIT_FLIPS = BANK_WORDS // P
+UNIT_K = 2 * BANK_WORDS
+UNIT_PASSES = UNIT_K // K_PASS
+UNIT_CHANNELS = UNIT_K // (KH * KW)
+UNIT_X = UNIT_CHANNELS * HEIGHT * WIDTH
+ROUND_UNITS = 2
+CHUNK_CHANNELS = ROUND_UNITS * UNIT_CHANNELS
+CHUNKS = CHANNELS // CHUNK_CHANNELS
 ROUNDS = CHUNKS * POSITIONS
 
+VECTOR_EVERY = 16
+
 FLOPS = 2 * POSITIONS * P * P * CHANNELS * KH * KW
-
-
-def flip(nc, banks, identity, rows, grouped):
-    row_words = rows[:].bitcast(F32)
-    grouped_words = grouped[:].bitcast(F32)
-    for n in range(ROUND_BANKS):
-        bank = banks.tile([P, BANK_FLIPS, P], F32)
-        for f in range(BANK_FLIPS):
-            first = (n * BANK_FLIPS + f) * P
-            nc.tensor.transpose(bank[:, f, :], row_words[:, first : first + P], identity[:])
-        nc.scalar.copy(
-            out=grouped_words[:, n * BANK_WORDS : (n + 1) * BANK_WORDS].rearrange(
-                "p (g c h) -> p g c h", g=BANK_PASSES, h=2
-            ),
-            in_=bank[:].rearrange("p (g h) c -> p g c h", h=2),
-        )
-
-
-def quantise(nc, pool, grouped, label):
-    codes = pool.tile([P, CHUNK_K // 4], U32, name=label + "_codes", tag=label + "_codes", align_bytes=64)
-    scales = pool.tile([P, CHUNK_K // 4], U8, name=label + "_scales", tag=label + "_scales", align_bytes=64)
-    nc.vector.quantize_mx(out=codes[:].bitcast(FP8X4), scales=scales[:], in_=grouped[:])
-    return codes, scales
 
 
 def tile_localconvolution_k_kernel(tc, x, weight, out):
@@ -62,9 +41,9 @@ def tile_localconvolution_k_kernel(tc, x, weight, out):
     with ExitStack() as ctx:
         const = ctx.enter_context(tc.tile_pool(name="const", bufs=1))
         inputs = ctx.enter_context(tc.tile_pool(name="inputs", bufs=1))
-        patches = ctx.enter_context(tc.tile_pool(name="patches", bufs=3))
-        regrouped = ctx.enter_context(tc.tile_pool(name="regrouped", bufs=2))
-        quantised = ctx.enter_context(tc.tile_pool(name="quantised", bufs=3))
+        patches = ctx.enter_context(tc.tile_pool(name="patches", bufs=3 * ROUND_UNITS))
+        regrouped = ctx.enter_context(tc.tile_pool(name="regrouped", bufs=2 * ROUND_UNITS))
+        quantised = ctx.enter_context(tc.tile_pool(name="quantised", bufs=3 * ROUND_UNITS))
         banks = ctx.enter_context(tc.psum_pool(name="banks", bufs=4))
         sums = ctx.enter_context(tc.psum_pool(name="sums", bufs=1))
         ctx.enter_context(tc.manual_schedule())
@@ -72,76 +51,115 @@ def tile_localconvolution_k_kernel(tc, x, weight, out):
         identity = const.tile([P, P], F32)
         make_identity(nc, identity[:])
 
-        x_chunks = []
-        w_chunks = []
+        x_units = []
+        w_rounds = []
+
+        def load_x(c, n):
+            first = c * CHUNK_CHANNELS + n * UNIT_CHANNELS
+            x_sb = inputs.tile([P, UNIT_X], BF16, name="x%d_%d" % (c, n))
+            nc.sync.dma_start(
+                out=x_sb[:], in_=x[:, first : first + UNIT_CHANNELS, :, :].rearrange("b c h w -> b (c h w)")
+            )
+            x_units.append(x_sb)
+
+        def load_w(c, q):
+            first = c * CHUNK_CHANNELS
+            w_sb = inputs.tile([P, ROUND_UNITS * UNIT_K], BF16, name="w%d_%d" % (c, q))
+            nc.sync.dma_start(
+                out=w_sb[:],
+                in_=weight[q // COLS, q % COLS, :, first : first + CHUNK_CHANNELS, :, :].rearrange(
+                    "o c u v -> o (c u v)"
+                ),
+            )
+            w_rounds.append(w_sb)
+
         for c in range(CHUNKS):
-            channels = slice(c * CHUNK_CHANNELS, (c + 1) * CHUNK_CHANNELS)
-            x_sb = inputs.tile([P, CHUNK_X], BF16, name="x%d" % c)
-            nc.sync.dma_start(out=x_sb[:], in_=x[:, channels, :, :].rearrange("b c h w -> b (c h w)"))
-            x_chunks.append(x_sb)
-            for q in range(POSITIONS):
-                w_sb = inputs.tile([P, CHUNK_K], BF16, name="w%d_%d" % (c, q))
-                nc.sync.dma_start(
-                    out=w_sb[:],
-                    in_=weight[q // COLS, q % COLS, :, channels, :, :].rearrange("o c u v -> o (c u v)"),
-                )
-                w_chunks.append(w_sb)
+            load_x(c, 0)
+            load_w(c, 0)
+            load_x(c, 1)
+            for q in range(1, POSITIONS):
+                load_w(c, q)
 
         totals = [sums.tile([P, P], F32, name="total%d" % q) for q in range(POSITIONS)]
         planes = const.tile([P, POSITIONS, P], F32)
 
-        def gather(r):
+        def gather(r, n):
             i = (r % POSITIONS) // COLS
             j = (r % POSITIONS) % COLS
-            patch = patches.tile([P, CHUNK_K], BF16)
+            patch = patches.tile([P, UNIT_K], BF16)
             nc.vector.tensor_copy(
                 out=patch[:].rearrange("b (c u v) -> b c u v", u=KH, v=KW),
-                in_=x_chunks[r // POSITIONS][:].rearrange("b (c h w) -> b c h w", h=HEIGHT, w=WIDTH)[
-                    :, :, i : i + KH, j : j + KW
-                ],
+                in_=x_units[(r // POSITIONS) * ROUND_UNITS + n][:].rearrange(
+                    "b (c h w) -> b c h w", h=HEIGHT, w=WIDTH
+                )[:, :, i : i + KH, j : j + KW],
             )
             return patch
 
-        def transpose(r, patch):
-            w_grouped = regrouped.tile([P, CHUNK_K], BF16, align_bytes=64)
-            flip(nc, banks, identity, w_chunks[r], w_grouped)
-            x_grouped = regrouped.tile([P, CHUNK_K], BF16, align_bytes=64)
-            flip(nc, banks, identity, patch, x_grouped)
-            return x_grouped, w_grouped
+        def flip(rows, label, bank_index):
+            row_words = rows.bitcast(F32)
+            bank = banks.tile([P, UNIT_FLIPS, P], F32)
+            for f in range(UNIT_FLIPS):
+                nc.tensor.transpose(bank[:, f, :], row_words[:, f * P : (f + 1) * P], identity[:])
+            grouped = regrouped.tile(
+                [P, UNIT_K], BF16, name=label + "_grouped", tag=label + "_grouped", align_bytes=64
+            )
+            target = grouped[:].bitcast(F32).rearrange("p (g c h) -> p g c h", g=UNIT_PASSES, h=2)
+            source = bank[:].rearrange("p (g h) c -> p g c h", h=2)
+            if bank_index % VECTOR_EVERY == VECTOR_EVERY // 2:
+                nc.vector.tensor_copy(out=target, in_=source)
+            else:
+                nc.scalar.copy(out=target, in_=source)
+            return grouped
 
-        def multiply(r, x_mx, w_mx):
-            x_codes, x_scales = x_mx
-            w_codes, w_scales = w_mx
-            for g in range(PASSES):
-                cols = slice(g * P, (g + 1) * P)
-                nc.tensor.matmul_mx(
-                    out=totals[r % POSITIONS][:],
-                    lhsT=x_codes[:, cols].bitcast(FP8X4),
-                    lhsT_scale=x_scales[:, cols],
-                    rhs=w_codes[:, cols].bitcast(FP8X4),
-                    rhs_scale=w_scales[:, cols],
-                    start=(r // POSITIONS == 0 and g == 0),
-                    stop=(r // POSITIONS == CHUNKS - 1 and g == PASSES - 1),
-                )
-            if r // POSITIONS == CHUNKS - 1:
-                nc.vector.tensor_copy(out=planes[:, r % POSITIONS, :], in_=totals[r % POSITIONS][:])
+        def quantise(grouped, label):
+            codes = quantised.tile(
+                [P, UNIT_K // 4], U32, name=label + "_codes", tag=label + "_codes", align_bytes=64
+            )
+            scales = quantised.tile(
+                [P, UNIT_K // 4], U8, name=label + "_scales", tag=label + "_scales", align_bytes=64
+            )
+            nc.vector.quantize_mx(out=codes[:].bitcast(FP8X4), scales=scales[:], in_=grouped[:])
+            return codes, scales
 
-        patch_of = {0: gather(0)}
+        def multiply(r, units):
+            total = totals[r % POSITIONS]
+            first_round = r // POSITIONS == 0
+            last_round = r // POSITIONS == CHUNKS - 1
+            for n in range(ROUND_UNITS):
+                (x_codes, x_scales), (w_codes, w_scales) = units[n]
+                for g in range(UNIT_PASSES):
+                    cols = slice(g * P, (g + 1) * P)
+                    nc.tensor.matmul_mx(
+                        out=total[:],
+                        lhsT=x_codes[:, cols].bitcast(FP8X4),
+                        lhsT_scale=x_scales[:, cols],
+                        rhs=w_codes[:, cols].bitcast(FP8X4),
+                        rhs_scale=w_scales[:, cols],
+                        start=(first_round and n == 0 and g == 0),
+                        stop=(last_round and n == ROUND_UNITS - 1 and g == UNIT_PASSES - 1),
+                    )
+            if last_round:
+                nc.vector.tensor_copy(out=planes[:, r % POSITIONS, :], in_=total[:])
+
+        patch_of = {0: [gather(0, n) for n in range(ROUND_UNITS)]}
         grouped_of = {}
         mx_of = {}
         for s in range(ROUNDS + 2):
             if s + 1 < ROUNDS:
-                patch_of[s + 1] = gather(s + 1)
+                patch_of[s + 1] = [gather(s + 1, n) for n in range(ROUND_UNITS)]
             if s < ROUNDS:
-                grouped_of[s] = transpose(s, patch_of[s])
+                grouped_of[s] = []
+                for n in range(ROUND_UNITS):
+                    bank_index = 2 * (s * ROUND_UNITS + n)
+                    x_grouped = flip(patch_of[s][n][:], "x", bank_index)
+                    w_grouped = flip(w_rounds[s][:, n * UNIT_K : (n + 1) * UNIT_K], "w", bank_index + 1)
+                    grouped_of[s].append((x_grouped, w_grouped))
             if 1 <= s <= ROUNDS:
-                x_grouped, w_grouped = grouped_of[s - 1]
-                w_mx = quantise(nc, quantised, w_grouped, "w")
-                x_mx = quantise(nc, quantised, x_grouped, "x")
-                mx_of[s - 1] = (x_mx, w_mx)
+                mx_of[s - 1] = [
+                    (quantise(x_grouped, "x"), quantise(w_grouped, "w")) for x_grouped, w_grouped in grouped_of[s - 1]
+                ]
             if s >= 2:
-                x_mx, w_mx = mx_of[s - 2]
-                multiply(s - 2, x_mx, w_mx)
+                multiply(s - 2, mx_of[s - 2])
 
         result = const.tile([P, P, POSITIONS], F32)
         nc.vector.tensor_copy(out=result[:], in_=planes[:].rearrange("b q o -> b o q"))

@@ -32,6 +32,7 @@ CHUNKS = CHANNELS // CHUNK_CHANNELS
 ROUNDS = CHUNKS * POSITIONS
 
 VECTOR_EVERY = 16
+FIRST_VECTOR_BANK = 8
 
 FLOPS = 2 * POSITIONS * P * P * CHANNELS * KH * KW
 
@@ -42,7 +43,7 @@ def tile_localconvolution_k_kernel(tc, x, weight, out):
         const = ctx.enter_context(tc.tile_pool(name="const", bufs=1))
         inputs = ctx.enter_context(tc.tile_pool(name="inputs", bufs=1))
         patches = ctx.enter_context(tc.tile_pool(name="patches", bufs=3 * ROUND_UNITS))
-        regrouped = ctx.enter_context(tc.tile_pool(name="regrouped", bufs=2 * ROUND_UNITS))
+        regrouped = ctx.enter_context(tc.tile_pool(name="regrouped", bufs=3 * ROUND_UNITS))
         quantised = ctx.enter_context(tc.tile_pool(name="quantised", bufs=3 * ROUND_UNITS))
         banks = ctx.enter_context(tc.psum_pool(name="banks", bufs=4))
         sums = ctx.enter_context(tc.psum_pool(name="sums", bufs=1))
@@ -95,30 +96,22 @@ def tile_localconvolution_k_kernel(tc, x, weight, out):
             )
             return patch
 
-        def flip(rows, label, bank_index):
+        def flip(rows, grouped, bank_index):
             row_words = rows.bitcast(F32)
             bank = banks.tile([P, UNIT_FLIPS, P], F32)
             for f in range(UNIT_FLIPS):
                 nc.tensor.transpose(bank[:, f, :], row_words[:, f * P : (f + 1) * P], identity[:])
-            grouped = regrouped.tile(
-                [P, UNIT_K], BF16, name=label + "_grouped", tag=label + "_grouped", align_bytes=64
-            )
-            target = grouped[:].bitcast(F32).rearrange("p (g c h) -> p g c h", g=UNIT_PASSES, h=2)
+            target = grouped.bitcast(F32).rearrange("p (g c h) -> p g c h", g=UNIT_PASSES, h=2)
             source = bank[:].rearrange("p (g h) c -> p g c h", h=2)
-            if bank_index % VECTOR_EVERY == VECTOR_EVERY // 2:
+            if bank_index % VECTOR_EVERY == FIRST_VECTOR_BANK:
                 nc.vector.tensor_copy(out=target, in_=source)
             else:
                 nc.scalar.copy(out=target, in_=source)
-            return grouped
 
-        def quantise(grouped, label):
-            codes = quantised.tile(
-                [P, UNIT_K // 4], U32, name=label + "_codes", tag=label + "_codes", align_bytes=64
-            )
-            scales = quantised.tile(
-                [P, UNIT_K // 4], U8, name=label + "_scales", tag=label + "_scales", align_bytes=64
-            )
-            nc.vector.quantize_mx(out=codes[:].bitcast(FP8X4), scales=scales[:], in_=grouped[:])
+        def quantise(pair):
+            codes = quantised.tile([P, 2 * UNIT_K // 4], U32, align_bytes=64)
+            scales = quantised.tile([P, 2 * UNIT_K // 4], U8, align_bytes=64)
+            nc.vector.quantize_mx(out=codes[:].bitcast(FP8X4), scales=scales[:], in_=pair[:])
             return codes, scales
 
         def multiply(r, units):
@@ -126,15 +119,16 @@ def tile_localconvolution_k_kernel(tc, x, weight, out):
             first_round = r // POSITIONS == 0
             last_round = r // POSITIONS == CHUNKS - 1
             for n in range(ROUND_UNITS):
-                (x_codes, x_scales), (w_codes, w_scales) = units[n]
+                codes, scales = units[n]
                 for g in range(UNIT_PASSES):
-                    cols = slice(g * P, (g + 1) * P)
+                    x_cols = slice(g * P, (g + 1) * P)
+                    w_cols = slice((UNIT_PASSES + g) * P, (UNIT_PASSES + g + 1) * P)
                     nc.tensor.matmul_mx(
                         out=total[:],
-                        lhsT=x_codes[:, cols].bitcast(FP8X4),
-                        lhsT_scale=x_scales[:, cols],
-                        rhs=w_codes[:, cols].bitcast(FP8X4),
-                        rhs_scale=w_scales[:, cols],
+                        lhsT=codes[:, x_cols].bitcast(FP8X4),
+                        lhsT_scale=scales[:, x_cols],
+                        rhs=codes[:, w_cols].bitcast(FP8X4),
+                        rhs_scale=scales[:, w_cols],
                         start=(first_round and n == 0 and g == 0),
                         stop=(last_round and n == ROUND_UNITS - 1 and g == UNIT_PASSES - 1),
                     )
@@ -151,13 +145,12 @@ def tile_localconvolution_k_kernel(tc, x, weight, out):
                 grouped_of[s] = []
                 for n in range(ROUND_UNITS):
                     bank_index = 2 * (s * ROUND_UNITS + n)
-                    x_grouped = flip(patch_of[s][n][:], "x", bank_index)
-                    w_grouped = flip(w_rounds[s][:, n * UNIT_K : (n + 1) * UNIT_K], "w", bank_index + 1)
-                    grouped_of[s].append((x_grouped, w_grouped))
+                    pair = regrouped.tile([P, 2 * UNIT_K], BF16, align_bytes=64)
+                    flip(patch_of[s][n][:], pair[:, :UNIT_K], bank_index)
+                    flip(w_rounds[s][:, n * UNIT_K : (n + 1) * UNIT_K], pair[:, UNIT_K:], bank_index + 1)
+                    grouped_of[s].append(pair)
             if 1 <= s <= ROUNDS:
-                mx_of[s - 1] = [
-                    (quantise(x_grouped, "x"), quantise(w_grouped, "w")) for x_grouped, w_grouped in grouped_of[s - 1]
-                ]
+                mx_of[s - 1] = [quantise(pair) for pair in grouped_of[s - 1]]
             if s >= 2:
                 multiply(s - 2, mx_of[s - 2])
 

from contextlib import ExitStack

import concourse.mybir as mybir
from concourse.masks import make_identity

BF16 = mybir.dt.bfloat16
F32 = mybir.dt.float32
U32 = mybir.dt.uint32
U8 = mybir.dt.uint8
FP8X4 = mybir.dt.float8_e4m3fn_x4

P = 128
CHANNELS = 1024
ROWS = 2
COLS = 2
KH = 4
KW = 4
HEIGHT = ROWS + KH - 1
WIDTH = COLS + KW - 1
POSITIONS = ROWS * COLS

K_PASS = 4 * P
BANK_WORDS = 512
UNIT_FLIPS = BANK_WORDS // P
UNIT_K = 2 * BANK_WORDS
UNIT_PASSES = UNIT_K // K_PASS
UNIT_CHANNELS = UNIT_K // (KH * KW)
UNIT_X = UNIT_CHANNELS * HEIGHT * WIDTH
ROUND_UNITS = 2
CHUNK_CHANNELS = ROUND_UNITS * UNIT_CHANNELS
CHUNKS = CHANNELS // CHUNK_CHANNELS
ROUNDS = CHUNKS * POSITIONS

VECTOR_EVERY = 16
FIRST_VECTOR_BANK = 8

FLOPS = 2 * POSITIONS * P * P * CHANNELS * KH * KW


def tile_localconvolution_k_kernel(tc, x, weight, out):
    nc = tc.nc
    with ExitStack() as ctx:
        const = ctx.enter_context(tc.tile_pool(name="const", bufs=1))
        inputs = ctx.enter_context(tc.tile_pool(name="inputs", bufs=1))
        patches = ctx.enter_context(tc.tile_pool(name="patches", bufs=3 * ROUND_UNITS))
        regrouped = ctx.enter_context(tc.tile_pool(name="regrouped", bufs=3 * ROUND_UNITS))
        quantised = ctx.enter_context(tc.tile_pool(name="quantised", bufs=3 * ROUND_UNITS))
        banks = ctx.enter_context(tc.psum_pool(name="banks", bufs=4))
        sums = ctx.enter_context(tc.psum_pool(name="sums", bufs=1))
        ctx.enter_context(tc.manual_schedule())

        identity = const.tile([P, P], F32)
        make_identity(nc, identity[:])

        x_units = []
        w_rounds = []

        def load_x(c, n):
            first = c * CHUNK_CHANNELS + n * UNIT_CHANNELS
            x_sb = inputs.tile([P, UNIT_X], BF16, name="x%d_%d" % (c, n))
            nc.sync.dma_start(
                out=x_sb[:], in_=x[:, first : first + UNIT_CHANNELS, :, :].rearrange("b c h w -> b (c h w)")
            )
            x_units.append(x_sb)

        def load_w(c, q):
            first = c * CHUNK_CHANNELS
            w_sb = inputs.tile([P, ROUND_UNITS * UNIT_K], BF16, name="w%d_%d" % (c, q))
            nc.sync.dma_start(
                out=w_sb[:],
                in_=weight[q // COLS, q % COLS, :, first : first + CHUNK_CHANNELS, :, :].rearrange(
                    "o c u v -> o (c u v)"
                ),
            )
            w_rounds.append(w_sb)

        for c in range(CHUNKS):
            load_x(c, 0)
            load_w(c, 0)
            load_x(c, 1)
            for q in range(1, POSITIONS):
                load_w(c, q)

        totals = [sums.tile([P, P], F32, name="total%d" % q) for q in range(POSITIONS)]
        planes = const.tile([P, POSITIONS, P], F32)

        def gather(r, n):
            i = (r % POSITIONS) // COLS
            j = (r % POSITIONS) % COLS
            patch = patches.tile([P, UNIT_K], BF16)
            nc.vector.tensor_copy(
                out=patch[:].rearrange("b (c u v) -> b c u v", u=KH, v=KW),
                in_=x_units[(r // POSITIONS) * ROUND_UNITS + n][:].rearrange(
                    "b (c h w) -> b c h w", h=HEIGHT, w=WIDTH
                )[:, :, i : i + KH, j : j + KW],
            )
            return patch

        def flip(rows, grouped, bank_index):
            row_words = rows.bitcast(F32)
            bank = banks.tile([P, UNIT_FLIPS, P], F32)
            for f in range(UNIT_FLIPS):
                nc.tensor.transpose(bank[:, f, :], row_words[:, f * P : (f + 1) * P], identity[:])
            target = grouped.bitcast(F32).rearrange("p (g c h) -> p g c h", g=UNIT_PASSES, h=2)
            source = bank[:].rearrange("p (g h) c -> p g c h", h=2)
            if bank_index % VECTOR_EVERY == FIRST_VECTOR_BANK:
                nc.vector.tensor_copy(out=target, in_=source)
            else:
                nc.scalar.copy(out=target, in_=source)

        def quantise(pair):
            codes = quantised.tile([P, 2 * UNIT_K // 4], U32, align_bytes=64)
            scales = quantised.tile([P, 2 * UNIT_K // 4], U8, align_bytes=64)
            nc.vector.quantize_mx(out=codes[:].bitcast(FP8X4), scales=scales[:], in_=pair[:])
            return codes, scales

        def multiply(r, units):
            total = totals[r % POSITIONS]
            first_round = r // POSITIONS == 0
            last_round = r // POSITIONS == CHUNKS - 1
            for n in range(ROUND_UNITS):
                codes, scales = units[n]
                for g in range(UNIT_PASSES):
                    x_cols = slice(g * P, (g + 1) * P)
                    w_cols = slice((UNIT_PASSES + g) * P, (UNIT_PASSES + g + 1) * P)
                    nc.tensor.matmul_mx(
                        out=total[:],
                        lhsT=codes[:, x_cols].bitcast(FP8X4),
                        lhsT_scale=scales[:, x_cols],
                        rhs=codes[:, w_cols].bitcast(FP8X4),
                        rhs_scale=scales[:, w_cols],
                        start=(first_round and n == 0 and g == 0),
                        stop=(last_round and n == ROUND_UNITS - 1 and g == UNIT_PASSES - 1),
                    )
            if last_round:
                nc.vector.tensor_copy(out=planes[:, r % POSITIONS, :], in_=total[:])

        patch_of = {0: [gather(0, n) for n in range(ROUND_UNITS)]}
        grouped_of = {}
        mx_of = {}
        for s in range(ROUNDS + 2):
            if s + 1 < ROUNDS:
                patch_of[s + 1] = [gather(s + 1, n) for n in range(ROUND_UNITS)]
            if s < ROUNDS:
                grouped_of[s] = []
                for n in range(ROUND_UNITS):
                    bank_index = 2 * (s * ROUND_UNITS + n)
                    pair = regrouped.tile([P, 2 * UNIT_K], BF16, align_bytes=64)
                    flip(patch_of[s][n][:], pair[:, :UNIT_K], bank_index)
                    flip(w_rounds[s][:, n * UNIT_K : (n + 1) * UNIT_K], pair[:, UNIT_K:], bank_index + 1)
                    grouped_of[s].append(pair)
            if 1 <= s <= ROUNDS:
                mx_of[s - 1] = [quantise(pair) for pair in grouped_of[s - 1]]
            if s >= 2:
                multiply(s - 2, mx_of[s - 2])

        result = const.tile([P, P, POSITIONS], F32)
        nc.vector.tensor_copy(out=result[:], in_=planes[:].rearrange("b q o -> b o q"))
        nc.sync.dma_start(out=out.rearrange("b o i j -> b (o i j)"), in_=result[:].rearrange("b o q -> b (o q)"))
